import numpy as np
import ml_dtypes


def mxq(x, axis, fmt="e4m3"):
    dtype, down = {"e4m3": (ml_dtypes.float8_e4m3fn, 7), "e5m2": (ml_dtypes.float8_e5m2, 14)}[fmt]
    v = np.moveaxis(np.asarray(x, np.float32).astype(ml_dtypes.bfloat16).astype(np.float64), axis, -1)
    blocks = v.reshape(v.shape[:-1] + (-1, 32))
    amax = np.abs(blocks).max(-1, keepdims=True)
    byte = np.maximum(np.where(amax > 0, np.frexp(amax)[1] - 1 + 127, 0) - down, 1)
    scale = np.exp2(byte - 127.0)
    codes = (blocks / scale).astype(np.float32).astype(dtype).astype(np.float64)
    return np.moveaxis((codes * scale).reshape(v.shape), -1, axis)


WIDE = False


def mx_kscale(k):
    if not WIDE:
        return np.ones(k)
    levels = np.array([10, -10, 5, -5, 0])
    a = np.random.permutation(np.resize(levels, k // 512 * 4)).reshape(k // 512, 4)
    idx = np.arange(k)
    return np.exp2(a[idx // 512, idx % 128 // 32])


BF16 = ml_dtypes.bfloat16


def bf(x):
    return np.asarray(x, np.float32).astype(BF16)


def f64(x):
    return np.asarray(x).astype(np.float64)


B, N, NIN, CTX, H, NOUT = 2, 512, 512, 3, 1024, 2
F = NIN * CTX


def shift_down(y, d):
    return np.pad(y[:, :-d, :], ((0, 0), (d, 0), (0, 0)))


def shift_up(y, d):
    return np.pad(y[:, d:, :], ((0, 0), (0, d), (0, 0)))


def context_linear(xq, w, shifts):
    y = xq @ mxq(w[:, :NIN].T, 0, "e4m3")
    c = 1
    for d in range(1, CTX // 2 + 1):
        for shift in shifts:
            y = y + shift(xq @ mxq(w[:, c * NIN:(c + 1) * NIN].T, 0, "e4m3"), d)
            c += 1
    return y


def setup_inputs():
    s, u = mx_kscale(NIN), mx_kscale(H)
    return {"t_bil": bf(np.random.standard_normal((B, N, NOUT, H)) * 0.15 / u),
            "x_r": bf(np.random.standard_normal((B, N, NIN)) * s),
            "W_r": bf(np.random.standard_normal((H, F)) / np.sqrt(F) / np.tile(s, CTX) * u[:, None]),
            "b_r": bf(np.random.standard_normal(H) * 0.3 * u),
            "b_bil": bf(np.random.standard_normal(NOUT))}


def reference(t_bil, x_r, W_r, b_r, b_bil):
    xq = mxq(f64(x_r), 2, "e4m3")
    hr = np.maximum(context_linear(xq, f64(W_r), (shift_up, shift_down)) + f64(b_r), 0.0)
    tq = mxq(f64(t_bil).reshape(B, N * NOUT, H), 2, "e4m3")
    sc = tq @ mxq(hr.transpose(0, 2, 1), 1, "e4m3")
    return sc.reshape(B, N, NOUT, N).transpose(0, 1, 3, 2) + f64(b_bil)

@@ -1,0 +1,205 @@
+from contextlib import ExitStack
+
+import concourse.mybir as mybir
+from concourse.masks import make_identity
+
+BF16 = mybir.dt.bfloat16
+F32 = mybir.dt.float32
+U32 = mybir.dt.uint32
+U8 = mybir.dt.uint8
+FP8X4 = mybir.dt.float8_e4m3fn_x4
+RELU = mybir.ActivationFunctionType.Relu
+ADD = mybir.AluOpType.add
+
+BATCH, POS, FEAT, TAPS, HID, NOUT = 2, 512, 512, 3, 1024, 2
+FLOPS = 2 * BATCH * POS * TAPS * FEAT * HID + 2 * BATCH * POS * NOUT * POS * HID
+
+P = 128
+PACK = 4
+K_PASS = P * PACK
+HALVES = 2
+PASS_WORDS = HALVES * P
+UNIT_BLOCKS = 2
+UNIT_COLS = UNIT_BLOCKS * P
+STRIDE = POS // P
+GROUPS = STRIDE + 2
+TAP_SHIFT = (0, 1, -1)
+W_TILES = HID // (2 * P)
+HID_PASSES = HID // K_PASS
+POS_TILES = POS // P
+HALF_POS = POS // 2
+
+
+def tile_bilinearpairedlayer_pb_kernel(tc, t_bil, x_r, W_r, b_r, b_bil, out):
+    nc = tc.nc
+    with ExitStack() as ctx:
+        keep = ctx.enter_context(tc.tile_pool(name="keep", bufs=1))
+        work = ctx.enter_context(tc.tile_pool(name="work", bufs=4))
+        psum_t = ctx.enter_context(tc.psum_pool(name="psum_t", bufs=4))
+        psum_acc = ctx.enter_context(tc.psum_pool(name="psum_acc", bufs=4))
+
+        b_r_bf = keep.tile([P, W_TILES, 2], BF16)
+        nc.scalar.dma_start(out=b_r_bf[:], in_=b_r.rearrange("(a p e) -> p a e", p=P, e=2))
+        b_bil_bf = keep.tile([P, NOUT], BF16)
+        nc.scalar.dma_start(out=b_bil_bf[:], in_=b_bil.partition_broadcast(P))
+
+        x_sb = [keep.tile([P, STRIDE * FEAT], BF16, name="x_sb%d" % b) for b in range(BATCH)]
+        w_sb = [keep.tile([P, 2 * TAPS * FEAT], BF16, name="w_sb%d" % a) for a in range(W_TILES)]
+        t_sb = [
+            [keep.tile([P, NOUT * HID], BF16, name="t_sb%d_%d" % (b, c)) for c in range(POS_TILES)]
+            for b in range(BATCH)
+        ]
+        w_rows = W_r.rearrange("(a p e) c -> a p (e c)", p=P, e=2)
+
+        def load_x(b):
+            nc.sync.dma_start(out=x_sb[b][:], in_=x_r[b].rearrange("(q r) f -> q (r f)", r=STRIDE))
+
+        load_x(0)
+        for a in range(W_TILES):
+            nc.sync.dma_start(out=w_sb[a][:], in_=w_rows[a])
+        load_x(1)
+        for b in range(BATCH):
+            t_rows = t_bil[b].rearrange("(c p) k g -> c p (k g)", p=P)
+            for c in range(POS_TILES):
+                nc.sync.dma_start(out=t_sb[b][c][:], in_=t_rows[c])
+
+        ident = keep.tile([P, P], F32)
+        make_identity(nc, ident[:])
+        bias_h = keep.tile([P, W_TILES * 2], F32)
+        nc.vector.tensor_copy(out=bias_h[:], in_=b_r_bf[:].rearrange("p a e -> p (a e)"))
+        bias_o = keep.tile([P, 2, NOUT], F32)
+        nc.vector.tensor_copy(out=bias_o[:], in_=b_bil_bf[:].unsqueeze(1).to_broadcast([P, 2, NOUT]))
+
+        x_grouped = [keep.tile([P, GROUPS * P * PACK], BF16, name="x_grouped%d" % b, align_bytes=64) for b in range(BATCH)]
+        x_codes = [keep.tile([P, GROUPS * P], U32, name="x_codes%d" % b, align_bytes=64) for b in range(BATCH)]
+        x_scales = [keep.tile([P, GROUPS * P], U8, name="x_scales%d" % b, align_bytes=64) for b in range(BATCH)]
+        w_codes = keep.tile([P, TAPS * HID], U32, align_bytes=64)
+        w_scales = keep.tile([P, TAPS * HID], U8, align_bytes=64)
+        t_codes = [keep.tile([P, NOUT * HID_PASSES * POS], U32, name="t_codes%d" % b, align_bytes=64) for b in range(BATCH)]
+        t_scales = [keep.tile([P, NOUT * HID_PASSES * POS], U8, name="t_scales%d" % b, align_bytes=64) for b in range(BATCH)]
+        h_rows = [[keep.tile([P, PACK, POS], BF16, name="h_rows%d_%d" % (b, g)) for g in range(HID_PASSES)] for b in range(BATCH)]
+        h_codes = [[keep.tile([P, POS], U32, name="h_codes%d_%d" % (b, g), align_bytes=64) for g in range(HID_PASSES)] for b in range(BATCH)]
+        h_scales = [[keep.tile([P, POS], U8, name="h_scales%d_%d" % (b, g), align_bytes=64) for g in range(HID_PASSES)] for b in range(BATCH)]
+
+        def transpose_unit(src, unit, copy, grouped):
+            words = src[:].bitcast(F32)
+            bank = psum_t.tile([P, HALVES, UNIT_COLS], F32, tag="bank")
+            for blk in range(UNIT_BLOCKS):
+                for u in range(HALVES):
+                    first = (unit * UNIT_BLOCKS + blk) * PASS_WORDS + u * P
+                    nc.tensor.transpose(bank[:, u, blk * P : (blk + 1) * P], words[:, first : first + P], ident[:])
+            copy(
+                out=grouped.bitcast(F32).rearrange("p (c u) -> p c u", u=HALVES),
+                in_=bank[:].rearrange("p u c -> p c u"),
+            )
+
+        def quantise_unit(src, unit, copy, codes, scales, first_col):
+            grouped = work.tile([P, UNIT_COLS * PACK], BF16, tag="grouped", align_bytes=64)
+            transpose_unit(src, unit, copy, grouped[:])
+            cols = slice(first_col, first_col + UNIT_COLS)
+            nc.vector.quantize_mx(out=codes[:, cols].bitcast(FP8X4), scales=scales[:, cols], in_=grouped[:])
+
+        def prepare_x(b):
+            grouped = x_grouped[b]
+            group = P * PACK
+            for unit in range(STRIDE // UNIT_BLOCKS):
+                first = (1 + unit * UNIT_BLOCKS) * group
+                transpose_unit(x_sb[b], unit, nc.scalar.copy, grouped[:, first : first + UNIT_BLOCKS * group])
+            nc.vector.memset(grouped[:, 0:PACK], 0.0)
+            nc.vector.tensor_copy(out=grouped[:, PACK:group], in_=grouped[:, 4 * group : 5 * group - PACK])
+            nc.vector.tensor_copy(out=grouped[:, 5 * group : 6 * group - PACK], in_=grouped[:, group + PACK : 2 * group])
+            nc.vector.memset(grouped[:, 6 * group - PACK : 6 * group], 0.0)
+            for lo, hi in ((0, 4), (4, 6)):
+                nc.vector.quantize_mx(
+                    out=x_codes[b][:, lo * P : hi * P].bitcast(FP8X4),
+                    scales=x_scales[b][:, lo * P : hi * P],
+                    in_=grouped[:, lo * group : hi * group],
+                )
+
+        def prepare_w(a):
+            for unit in range(2 * TAPS // UNIT_BLOCKS):
+                quantise_unit(w_sb[a], unit, nc.scalar.copy, w_codes, w_scales, (a * TAPS + unit) * UNIT_COLS)
+
+        def prepare_t(b):
+            for c in range(POS_TILES):
+                for k in range(NOUT):
+                    copy = nc.scalar.copy if k % 2 == 0 else nc.vector.tensor_copy
+                    quantise_unit(t_sb[b][c], k, copy, t_codes[b], t_scales[b], (c * NOUT + k) * UNIT_COLS)
+
+        def hidden(b, a):
+            for e in range(2):
+                chunk = 2 * a + e
+                acc = psum_acc.tile([P, POS], F32, tag="acc")
+                for tap in range(TAPS):
+                    w_cols = slice((chunk * TAPS + tap) * P, (chunk * TAPS + tap + 1) * P)
+                    x_cols = slice((1 + TAP_SHIFT[tap]) * P, (1 + TAP_SHIFT[tap]) * P + POS)
+                    nc.tensor.matmul_mx(
+                        out=acc[:],
+                        lhsT=w_codes[:, w_cols].bitcast(FP8X4),
+                        lhsT_scale=w_scales[:, w_cols],
+                        rhs=x_codes[b][:, x_cols].bitcast(FP8X4),
+                        rhs_scale=x_scales[b][:, x_cols],
+                        start=(tap == 0),
+                        stop=(tap == TAPS - 1),
+                    )
+                nc.scalar.activation(
+                    out=h_rows[b][chunk // PACK][:, chunk % PACK, :],
+                    in_=acc[:],
+                    func=RELU,
+                    bias=bias_h[:, chunk : chunk + 1],
+                    scale=1.0,
+                )
+
+        def quantise_hidden(b, g, copy):
+            grouped = work.tile([P, POS * PACK], BF16, tag="h_grouped", align_bytes=64)
+            copy(
+                out=grouped[:].rearrange("p (c i t) -> p c t i", i=4, t=PACK),
+                in_=h_rows[b][g][:].rearrange("p t (c i) -> p c t i", i=4),
+            )
+            nc.vector.quantize_mx(out=h_codes[b][g][:].bitcast(FP8X4), scales=h_scales[b][g][:], in_=grouped[:])
+
+        def scores(b):
+            out_rows = out[b].rearrange("(c p) j k -> c p (j k)", p=P)
+            for c in range(POS_TILES):
+                result = work.tile([P, POS * NOUT], F32, tag="result")
+                by_group = result[:].rearrange("p (q r k) -> p q r k", r=STRIDE, k=NOUT)
+                for half in range(2):
+                    bank = psum_acc.tile([P, NOUT, HALF_POS], F32, tag="acc")
+                    h_cols = slice(half * HALF_POS, (half + 1) * HALF_POS)
+                    for k in range(NOUT):
+                        for g in range(HID_PASSES):
+                            t_first = ((c * NOUT + k) * HID_PASSES + g) * P
+                            nc.tensor.matmul_mx(
+                                out=bank[:, k, :],
+                                lhsT=t_codes[b][:, t_first : t_first + P].bitcast(FP8X4),
+                                lhsT_scale=t_scales[b][:, t_first : t_first + P],
+                                rhs=h_codes[b][g][:, h_cols].bitcast(FP8X4),
+                                rhs_scale=h_scales[b][g][:, h_cols],
+                                start=(g == 0),
+                                stop=(g == HID_PASSES - 1),
+                            )
+                    nc.vector.tensor_tensor(
+                        out=by_group[:, :, 2 * half : 2 * half + 2, :],
+                        in0=bank[:].rearrange("p k (r q) -> p q r k", r=2),
+                        in1=bias_o[:].unsqueeze(1).to_broadcast([P, P, 2, NOUT]),
+                        op=ADD,
+                    )
+                nc.sync.dma_start(out=out_rows[c], in_=result[:])
+
+        prepare_x(0)
+        prepare_w(0)
+        for a in range(W_TILES):
+            if a + 1 < W_TILES:
+                prepare_w(a + 1)
+            hidden(0, a)
+            if a % 2 == 1:
+                quantise_hidden(0, a // 2, nc.vector.tensor_copy)
+        prepare_x(1)
+        prepare_t(0)
+        for a in range(W_TILES):
+            hidden(1, a)
+            if a % 2 == 1:
+                quantise_hidden(1, a // 2, nc.scalar.copy)
+        prepare_t(1)
+        for b in range(BATCH):
+            scores(b)

@@ -186,6 +186,7 @@ def tile_bilinearpairedlayer_pb_kernel(tc, t_bil, x_r, W_r, b_r, b_bil, out):
                     )
                 nc.sync.dma_start(out=out_rows[c], in_=result[:])
 
+        ctx.enter_context(tc.manual_schedule())
         prepare_x(0)
         prepare_w(0)
         for a in range(W_TILES):

@@ -9,6 +9,7 @@ U32 = mybir.dt.uint32
 U8 = mybir.dt.uint8
 FP8X4 = mybir.dt.float8_e4m3fn_x4
 RELU = mybir.ActivationFunctionType.Relu
+IDENTITY = mybir.ActivationFunctionType.Identity
 ADD = mybir.AluOpType.add
 
 BATCH, POS, FEAT, TAPS, HID, NOUT = 2, 512, 512, 3, 1024, 2
@@ -35,8 +36,7 @@ def tile_bilinearpairedlayer_pb_kernel(tc, t_bil, x_r, W_r, b_r, b_bil, out):
     with ExitStack() as ctx:
         keep = ctx.enter_context(tc.tile_pool(name="keep", bufs=1))
         work = ctx.enter_context(tc.tile_pool(name="work", bufs=4))
-        psum_t = ctx.enter_context(tc.psum_pool(name="psum_t", bufs=4))
-        psum_acc = ctx.enter_context(tc.psum_pool(name="psum_acc", bufs=4))
+        psum = ctx.enter_context(tc.psum_pool(name="psum", bufs=8))
 
         b_r_bf = keep.tile([P, W_TILES, 2], BF16)
         nc.scalar.dma_start(out=b_r_bf[:], in_=b_r.rearrange("(a p e) -> p a e", p=P, e=2))
@@ -83,7 +83,7 @@ def tile_bilinearpairedlayer_pb_kernel(tc, t_bil, x_r, W_r, b_r, b_bil, out):
 
         def transpose_unit(src, unit, copy, grouped):
             words = src[:].bitcast(F32)
-            bank = psum_t.tile([P, HALVES, UNIT_COLS], F32, tag="bank")
+            bank = psum.tile([P, HALVES, UNIT_COLS], F32, tag="bank")
             for blk in range(UNIT_BLOCKS):
                 for u in range(HALVES):
                     first = (unit * UNIT_BLOCKS + blk) * PASS_WORDS + u * P
@@ -93,11 +93,16 @@ def tile_bilinearpairedlayer_pb_kernel(tc, t_bil, x_r, W_r, b_r, b_bil, out):
                 in_=bank[:].rearrange("p u c -> p c u"),
             )
 
-        def quantise_unit(src, unit, copy, codes, scales, first_col):
-            grouped = work.tile([P, UNIT_COLS * PACK], BF16, tag="grouped", align_bytes=64)
-            transpose_unit(src, unit, copy, grouped[:])
-            cols = slice(first_col, first_col + UNIT_COLS)
-            nc.vector.quantize_mx(out=codes[:, cols].bitcast(FP8X4), scales=scales[:, cols], in_=grouped[:])
+        def quantise_tile(src, copies, codes, scales, first_col):
+            grouped = [
+                work.tile([P, UNIT_COLS * PACK], BF16, name="grouped%d" % unit, tag="grouped", bufs=6, align_bytes=64)
+                for unit in range(len(copies))
+            ]
+            for unit in range(len(copies)):
+                transpose_unit(src, unit, copies[unit], grouped[unit][:])
+            for unit in range(len(copies)):
+                cols = slice(first_col + unit * UNIT_COLS, first_col + (unit + 1) * UNIT_COLS)
+                nc.vector.quantize_mx(out=codes[:, cols].bitcast(FP8X4), scales=scales[:, cols], in_=grouped[unit][:])
 
         def prepare_x(b):
             grouped = x_grouped[b]
@@ -117,19 +122,17 @@ def tile_bilinearpairedlayer_pb_kernel(tc, t_bil, x_r, W_r, b_r, b_bil, out):
                 )
 
         def prepare_w(a):
-            for unit in range(2 * TAPS // UNIT_BLOCKS):
-                quantise_unit(w_sb[a], unit, nc.scalar.copy, w_codes, w_scales, (a * TAPS + unit) * UNIT_COLS)
+            copies = [nc.scalar.copy, nc.scalar.copy, nc.vector.tensor_copy]
+            quantise_tile(w_sb[a], copies, w_codes, w_scales, a * TAPS * UNIT_COLS)
 
-        def prepare_t(b):
-            for c in range(POS_TILES):
-                for k in range(NOUT):
-                    copy = nc.scalar.copy if k % 2 == 0 else nc.vector.tensor_copy
-                    quantise_unit(t_sb[b][c], k, copy, t_codes[b], t_scales[b], (c * NOUT + k) * UNIT_COLS)
+        def prepare_t(b, c):
+            last_copy = nc.vector.tensor_copy if c % 2 == 1 else nc.scalar.copy
+            quantise_tile(t_sb[b][c], [nc.scalar.copy, last_copy], t_codes[b], t_scales[b], c * NOUT * UNIT_COLS)
 
         def hidden(b, a):
             for e in range(2):
                 chunk = 2 * a + e
-                acc = psum_acc.tile([P, POS], F32, tag="acc")
+                acc = psum.tile([P, POS], F32, tag="bank")
                 for tap in range(TAPS):
                     w_cols = slice((chunk * TAPS + tap) * P, (chunk * TAPS + tap + 1) * P)
                     x_cols = slice((1 + TAP_SHIFT[tap]) * P, (1 + TAP_SHIFT[tap]) * P + POS)
@@ -151,7 +154,7 @@ def tile_bilinearpairedlayer_pb_kernel(tc, t_bil, x_r, W_r, b_r, b_bil, out):
                 )
 
         def quantise_hidden(b, g, copy):
-            grouped = work.tile([P, POS * PACK], BF16, tag="h_grouped", align_bytes=64)
+            grouped = work.tile([P, POS * PACK], BF16, tag="h_grouped", bufs=2, align_bytes=64)
             copy(
                 out=grouped[:].rearrange("p (c i t) -> p c t i", i=4, t=PACK),
                 in_=h_rows[b][g][:].rearrange("p t (c i) -> p c t i", i=4),
@@ -164,7 +167,7 @@ def tile_bilinearpairedlayer_pb_kernel(tc, t_bil, x_r, W_r, b_r, b_bil, out):
                 result = work.tile([P, POS * NOUT], F32, tag="result")
                 by_group = result[:].rearrange("p (q r k) -> p q r k", r=STRIDE, k=NOUT)
                 for half in range(2):
-                    bank = psum_acc.tile([P, NOUT, HALF_POS], F32, tag="acc")
+                    bank = psum.tile([P, NOUT, HALF_POS], F32, tag="bank")
                     h_cols = slice(half * HALF_POS, (half + 1) * HALF_POS)
                     for k in range(NOUT):
                         for g in range(HID_PASSES):
@@ -178,12 +181,23 @@ def tile_bilinearpairedlayer_pb_kernel(tc, t_bil, x_r, W_r, b_r, b_bil, out):
                                 start=(g == 0),
                                 stop=(g == HID_PASSES - 1),
                             )
-                    nc.vector.tensor_tensor(
-                        out=by_group[:, :, 2 * half : 2 * half + 2, :],
-                        in0=bank[:].rearrange("p k (r q) -> p q r k", r=2),
-                        in1=bias_o[:].unsqueeze(1).to_broadcast([P, P, 2, NOUT]),
-                        op=ADD,
-                    )
+                    groups = slice(2 * half, 2 * half + 2)
+                    if c == 0:
+                        for k in range(NOUT):
+                            nc.scalar.activation(
+                                out=by_group[:, :, groups, k],
+                                in_=bank[:, k, :].rearrange("p (r q) -> p q r", r=2),
+                                func=IDENTITY,
+                                bias=bias_o[:, 0, k : k + 1],
+                                scale=1.0,
+                            )
+                    else:
+                        nc.vector.tensor_tensor(
+                            out=by_group[:, :, groups, :],
+                            in0=bank[:].rearrange("p k (r q) -> p q r k", r=2),
+                            in1=bias_o[:].unsqueeze(1).to_broadcast([P, P, 2, NOUT]),
+                            op=ADD,
+                        )
                 nc.sync.dma_start(out=out_rows[c], in_=result[:])
 
         ctx.enter_context(tc.manual_schedule())
@@ -192,15 +206,16 @@ def tile_bilinearpairedlayer_pb_kernel(tc, t_bil, x_r, W_r, b_r, b_bil, out):
         for a in range(W_TILES):
             if a + 1 < W_TILES:
                 prepare_w(a + 1)
+            else:
+                prepare_x(1)
             hidden(0, a)
             if a % 2 == 1:
                 quantise_hidden(0, a // 2, nc.vector.tensor_copy)
-        prepare_x(1)
-        prepare_t(0)
         for a in range(W_TILES):
+            for t_tile in (2 * a, 2 * a + 1):
+                prepare_t(t_tile // POS_TILES, t_tile % POS_TILES)
             hidden(1, a)
             if a % 2 == 1:
-                quantise_hidden(1, a // 2, nc.scalar.copy)
-        prepare_t(1)
+                quantise_hidden(1, a // 2, nc.vector.tensor_copy)
         for b in range(BATCH):
             scores(b)

@@ -164,7 +164,7 @@ def tile_bilinearpairedlayer_pb_kernel(tc, t_bil, x_r, W_r, b_r, b_bil, out):
         def scores(b):
             out_rows = out[b].rearrange("(c p) j k -> c p (j k)", p=P)
             for c in range(POS_TILES):
-                result = work.tile([P, POS * NOUT], F32, tag="result")
+                result = work.tile([P, POS * NOUT], F32, tag="result", bufs=BATCH * POS_TILES)
                 by_group = result[:].rearrange("p (q r k) -> p q r k", r=STRIDE, k=NOUT)
                 for half in range(2):
                     bank = psum.tile([P, NOUT, HALF_POS], F32, tag="bank")

@@ -111,9 +111,9 @@ def tile_bilinearpairedlayer_pb_kernel(tc, t_bil, x_r, W_r, b_r, b_bil, out):
                 first = (1 + unit * UNIT_BLOCKS) * group
                 transpose_unit(x_sb[b], unit, nc.scalar.copy, grouped[:, first : first + UNIT_BLOCKS * group])
             nc.vector.memset(grouped[:, 0:PACK], 0.0)
+            nc.vector.memset(grouped[:, 6 * group - PACK : 6 * group], 0.0)
             nc.vector.tensor_copy(out=grouped[:, PACK:group], in_=grouped[:, 4 * group : 5 * group - PACK])
             nc.vector.tensor_copy(out=grouped[:, 5 * group : 6 * group - PACK], in_=grouped[:, group + PACK : 2 * group])
-            nc.vector.memset(grouped[:, 6 * group - PACK : 6 * group], 0.0)
             for lo, hi in ((0, 4), (4, 6)):
                 nc.vector.quantize_mx(
                     out=x_codes[b][:, lo * P : hi * P].bitcast(FP8X4),
@@ -155,11 +155,20 @@ def tile_bilinearpairedlayer_pb_kernel(tc, t_bil, x_r, W_r, b_r, b_bil, out):
 
         def quantise_hidden(b, g, copy):
             grouped = work.tile([P, POS * PACK], BF16, tag="h_grouped", bufs=2, align_bytes=64)
-            copy(
-                out=grouped[:].rearrange("p (c i t) -> p c t i", i=4, t=PACK),
-                in_=h_rows[b][g][:].rearrange("p t (c i) -> p c t i", i=4),
-            )
-            nc.vector.quantize_mx(out=h_codes[b][g][:].bitcast(FP8X4), scales=h_scales[b][g][:], in_=grouped[:])
+            for half in range(2):
+                copy(
+                    out=grouped[:, half * HALF_POS * PACK : (half + 1) * HALF_POS * PACK].rearrange(
+                        "p (c i t) -> p c t i", i=4, t=PACK
+                    ),
+                    in_=h_rows[b][g][:, :, half * HALF_POS : (half + 1) * HALF_POS].rearrange("p t (c i) -> p c t i", i=4),
+                )
+            for half in range(2):
+                cols = slice(half * HALF_POS, (half + 1) * HALF_POS)
+                nc.vector.quantize_mx(
+                    out=h_codes[b][g][:, cols].bitcast(FP8X4),
+                    scales=h_scales[b][g][:, cols],
+                    in_=grouped[:, half * HALF_POS * PACK : (half + 1) * HALF_POS * PACK],
+                )
 
         def scores(b):
             out_rows = out[b].rearrange("(c p) j k -> c p (j k)", p=P)

from contextlib import ExitStack

import concourse.mybir as mybir
from concourse.masks import make_identity

BF16 = mybir.dt.bfloat16
F32 = mybir.dt.float32
U32 = mybir.dt.uint32
U8 = mybir.dt.uint8
FP8X4 = mybir.dt.float8_e4m3fn_x4
RELU = mybir.ActivationFunctionType.Relu
IDENTITY = mybir.ActivationFunctionType.Identity
ADD = mybir.AluOpType.add

BATCH, POS, FEAT, TAPS, HID, NOUT = 2, 512, 512, 3, 1024, 2
FLOPS = 2 * BATCH * POS * TAPS * FEAT * HID + 2 * BATCH * POS * NOUT * POS * HID

P = 128
PACK = 4
K_PASS = P * PACK
HALVES = 2
PASS_WORDS = HALVES * P
UNIT_BLOCKS = 2
UNIT_COLS = UNIT_BLOCKS * P
STRIDE = POS // P
GROUPS = STRIDE + 2
TAP_SHIFT = (0, 1, -1)
W_TILES = HID // (2 * P)
HID_PASSES = HID // K_PASS
POS_TILES = POS // P
HALF_POS = POS // 2


def tile_bilinearpairedlayer_pb_kernel(tc, t_bil, x_r, W_r, b_r, b_bil, out):
    nc = tc.nc
    with ExitStack() as ctx:
        keep = ctx.enter_context(tc.tile_pool(name="keep", bufs=1))
        work = ctx.enter_context(tc.tile_pool(name="work", bufs=4))
        psum = ctx.enter_context(tc.psum_pool(name="psum", bufs=8))

        b_r_bf = keep.tile([P, W_TILES, 2], BF16)
        nc.scalar.dma_start(out=b_r_bf[:], in_=b_r.rearrange("(a p e) -> p a e", p=P, e=2))
        b_bil_bf = keep.tile([P, NOUT], BF16)
        nc.scalar.dma_start(out=b_bil_bf[:], in_=b_bil.partition_broadcast(P))

        x_sb = [keep.tile([P, STRIDE * FEAT], BF16, name="x_sb%d" % b) for b in range(BATCH)]
        w_sb = [keep.tile([P, 2 * TAPS * FEAT], BF16, name="w_sb%d" % a) for a in range(W_TILES)]
        t_sb = [
            [keep.tile([P, NOUT * HID], BF16, name="t_sb%d_%d" % (b, c)) for c in range(POS_TILES)]
            for b in range(BATCH)
        ]
        w_rows = W_r.rearrange("(a p e) c -> a p (e c)", p=P, e=2)

        def load_x(b):
            nc.sync.dma_start(out=x_sb[b][:], in_=x_r[b].rearrange("(q r) f -> q (r f)", r=STRIDE))

        load_x(0)
        for a in range(W_TILES):
            nc.sync.dma_start(out=w_sb[a][:], in_=w_rows[a])
        load_x(1)
        for b in range(BATCH):
            t_rows = t_bil[b].rearrange("(c p) k g -> c p (k g)", p=P)
            for c in range(POS_TILES):
                nc.sync.dma_start(out=t_sb[b][c][:], in_=t_rows[c])

        ident = keep.tile([P, P], F32)
        make_identity(nc, ident[:])
        bias_h = keep.tile([P, W_TILES * 2], F32)
        nc.vector.tensor_copy(out=bias_h[:], in_=b_r_bf[:].rearrange("p a e -> p (a e)"))
        bias_o = keep.tile([P, 2, NOUT], F32)
        nc.vector.tensor_copy(out=bias_o[:], in_=b_bil_bf[:].unsqueeze(1).to_broadcast([P, 2, NOUT]))

        x_grouped = [keep.tile([P, GROUPS * P * PACK], BF16, name="x_grouped%d" % b, align_bytes=64) for b in range(BATCH)]
        x_codes = [keep.tile([P, GROUPS * P], U32, name="x_codes%d" % b, align_bytes=64) for b in range(BATCH)]
        x_scales = [keep.tile([P, GROUPS * P], U8, name="x_scales%d" % b, align_bytes=64) for b in range(BATCH)]
        w_codes = keep.tile([P, TAPS * HID], U32, align_bytes=64)
        w_scales = keep.tile([P, TAPS * HID], U8, align_bytes=64)
        t_codes = [keep.tile([P, NOUT * HID_PASSES * POS], U32, name="t_codes%d" % b, align_bytes=64) for b in range(BATCH)]
        t_scales = [keep.tile([P, NOUT * HID_PASSES * POS], U8, name="t_scales%d" % b, align_bytes=64) for b in range(BATCH)]
        h_rows = [[keep.tile([P, PACK, POS], BF16, name="h_rows%d_%d" % (b, g)) for g in range(HID_PASSES)] for b in range(BATCH)]
        h_codes = [[keep.tile([P, POS], U32, name="h_codes%d_%d" % (b, g), align_bytes=64) for g in range(HID_PASSES)] for b in range(BATCH)]
        h_scales = [[keep.tile([P, POS], U8, name="h_scales%d_%d" % (b, g), align_bytes=64) for g in range(HID_PASSES)] for b in range(BATCH)]

        def transpose_unit(src, unit, copy, grouped):
            words = src[:].bitcast(F32)
            bank = psum.tile([P, HALVES, UNIT_COLS], F32, tag="bank")
            for blk in range(UNIT_BLOCKS):
                for u in range(HALVES):
                    first = (unit * UNIT_BLOCKS + blk) * PASS_WORDS + u * P
                    nc.tensor.transpose(bank[:, u, blk * P : (blk + 1) * P], words[:, first : first + P], ident[:])
            copy(
                out=grouped.bitcast(F32).rearrange("p (c u) -> p c u", u=HALVES),
                in_=bank[:].rearrange("p u c -> p c u"),
            )

        def quantise_tile(src, copies, codes, scales, first_col):
            grouped = [
                work.tile([P, UNIT_COLS * PACK], BF16, name="grouped%d" % unit, tag="grouped", bufs=6, align_bytes=64)
                for unit in range(len(copies))
            ]
            for unit in range(len(copies)):
                transpose_unit(src, unit, copies[unit], grouped[unit][:])
            for unit in range(len(copies)):
                cols = slice(first_col + unit * UNIT_COLS, first_col + (unit + 1) * UNIT_COLS)
                nc.vector.quantize_mx(out=codes[:, cols].bitcast(FP8X4), scales=scales[:, cols], in_=grouped[unit][:])

        def prepare_x(b):
            grouped = x_grouped[b]
            group = P * PACK
            for unit in range(STRIDE // UNIT_BLOCKS):
                first = (1 + unit * UNIT_BLOCKS) * group
                transpose_unit(x_sb[b], unit, nc.scalar.copy, grouped[:, first : first + UNIT_BLOCKS * group])
            nc.vector.memset(grouped[:, 0:PACK], 0.0)
            nc.vector.memset(grouped[:, 6 * group - PACK : 6 * group], 0.0)
            nc.vector.tensor_copy(out=grouped[:, PACK:group], in_=grouped[:, 4 * group : 5 * group - PACK])
            nc.vector.tensor_copy(out=grouped[:, 5 * group : 6 * group - PACK], in_=grouped[:, group + PACK : 2 * group])
            for lo, hi in ((0, 4), (4, 6)):
                nc.vector.quantize_mx(
                    out=x_codes[b][:, lo * P : hi * P].bitcast(FP8X4),
                    scales=x_scales[b][:, lo * P : hi * P],
                    in_=grouped[:, lo * group : hi * group],
                )

        def prepare_w(a):
            copies = [nc.scalar.copy, nc.scalar.copy, nc.vector.tensor_copy]
            quantise_tile(w_sb[a], copies, w_codes, w_scales, a * TAPS * UNIT_COLS)

        def prepare_t(b, c):
            last_copy = nc.vector.tensor_copy if c % 2 == 1 else nc.scalar.copy
            quantise_tile(t_sb[b][c], [nc.scalar.copy, last_copy], t_codes[b], t_scales[b], c * NOUT * UNIT_COLS)

        def hidden(b, a):
            for e in range(2):
                chunk = 2 * a + e
                acc = psum.tile([P, POS], F32, tag="bank")
                for tap in range(TAPS):
                    w_cols = slice((chunk * TAPS + tap) * P, (chunk * TAPS + tap + 1) * P)
                    x_cols = slice((1 + TAP_SHIFT[tap]) * P, (1 + TAP_SHIFT[tap]) * P + POS)
                    nc.tensor.matmul_mx(
                        out=acc[:],
                        lhsT=w_codes[:, w_cols].bitcast(FP8X4),
                        lhsT_scale=w_scales[:, w_cols],
                        rhs=x_codes[b][:, x_cols].bitcast(FP8X4),
                        rhs_scale=x_scales[b][:, x_cols],
                        start=(tap == 0),
                        stop=(tap == TAPS - 1),
                    )
                nc.scalar.activation(
                    out=h_rows[b][chunk // PACK][:, chunk % PACK, :],
                    in_=acc[:],
                    func=RELU,
                    bias=bias_h[:, chunk : chunk + 1],
                    scale=1.0,
                )

        def quantise_hidden(b, g, copy):
            grouped = work.tile([P, POS * PACK], BF16, tag="h_grouped", bufs=2, align_bytes=64)
            for half in range(2):
                copy(
                    out=grouped[:, half * HALF_POS * PACK : (half + 1) * HALF_POS * PACK].rearrange(
                        "p (c i t) -> p c t i", i=4, t=PACK
                    ),
                    in_=h_rows[b][g][:, :, half * HALF_POS : (half + 1) * HALF_POS].rearrange("p t (c i) -> p c t i", i=4),
                )
            for half in range(2):
                cols = slice(half * HALF_POS, (half + 1) * HALF_POS)
                nc.vector.quantize_mx(
                    out=h_codes[b][g][:, cols].bitcast(FP8X4),
                    scales=h_scales[b][g][:, cols],
                    in_=grouped[:, half * HALF_POS * PACK : (half + 1) * HALF_POS * PACK],
                )

        def scores(b):
            out_rows = out[b].rearrange("(c p) j k -> c p (j k)", p=P)
            for c in range(POS_TILES):
                result = work.tile([P, POS * NOUT], F32, tag="result", bufs=BATCH * POS_TILES)
                by_group = result[:].rearrange("p (q r k) -> p q r k", r=STRIDE, k=NOUT)
                for half in range(2):
                    bank = psum.tile([P, NOUT, HALF_POS], F32, tag="bank")
                    h_cols = slice(half * HALF_POS, (half + 1) * HALF_POS)
                    for k in range(NOUT):
                        for g in range(HID_PASSES):
                            t_first = ((c * NOUT + k) * HID_PASSES + g) * P
                            nc.tensor.matmul_mx(
                                out=bank[:, k, :],
                                lhsT=t_codes[b][:, t_first : t_first + P].bitcast(FP8X4),
                                lhsT_scale=t_scales[b][:, t_first : t_first + P],
                                rhs=h_codes[b][g][:, h_cols].bitcast(FP8X4),
                                rhs_scale=h_scales[b][g][:, h_cols],
                                start=(g == 0),
                                stop=(g == HID_PASSES - 1),
                            )
                    groups = slice(2 * half, 2 * half + 2)
                    if c == 0:
                        for k in range(NOUT):
                            nc.scalar.activation(
                                out=by_group[:, :, groups, k],
                                in_=bank[:, k, :].rearrange("p (r q) -> p q r", r=2),
                                func=IDENTITY,
                                bias=bias_o[:, 0, k : k + 1],
                                scale=1.0,
                            )
                    else:
                        nc.vector.tensor_tensor(
                            out=by_group[:, :, groups, :],
                            in0=bank[:].rearrange("p k (r q) -> p q r k", r=2),
                            in1=bias_o[:].unsqueeze(1).to_broadcast([P, P, 2, NOUT]),
                            op=ADD,
                        )
                nc.sync.dma_start(out=out_rows[c], in_=result[:])

        ctx.enter_context(tc.manual_schedule())
        prepare_x(0)
        prepare_w(0)
        for a in range(W_TILES):
            if a + 1 < W_TILES:
                prepare_w(a + 1)
            else:
                prepare_x(1)
            hidden(0, a)
            if a % 2 == 1:
                quantise_hidden(0, a // 2, nc.vector.tensor_copy)
        for a in range(W_TILES):
            for t_tile in (2 * a, 2 * a + 1):
                prepare_t(t_tile // POS_TILES, t_tile % POS_TILES)
            hidden(1, a)
            if a % 2 == 1:
                quantise_hidden(1, a // 2, nc.vector.tensor_copy)
        for b in range(BATCH):
            scores(b)
